import numpy as np
import ml_dtypes


def mxq(x, axis, fmt="e4m3"):
    dtype, down = {"e4m3": (ml_dtypes.float8_e4m3fn, 7), "e5m2": (ml_dtypes.float8_e5m2, 14)}[fmt]
    v = np.moveaxis(np.asarray(x, np.float32).astype(ml_dtypes.bfloat16).astype(np.float64), axis, -1)
    blocks = v.reshape(v.shape[:-1] + (-1, 32))
    amax = np.abs(blocks).max(-1, keepdims=True)
    byte = np.maximum(np.where(amax > 0, np.frexp(amax)[1] - 1 + 127, 0) - down, 1)
    scale = np.exp2(byte - 127.0)
    codes = (blocks / scale).astype(np.float32).astype(dtype).astype(np.float64)
    return np.moveaxis((codes * scale).reshape(v.shape), -1, axis)


WIDE = False


def mx_kscale(k):
    if not WIDE:
        return np.ones(k)
    levels = np.array([10, -10, 5, -5, 0])
    a = np.random.permutation(np.resize(levels, k // 512 * 4)).reshape(k // 512, 4)
    idx = np.arange(k)
    return np.exp2(a[idx // 512, idx % 128 // 32])


BF16 = ml_dtypes.bfloat16


def bf(x):
    return np.asarray(x, np.float32).astype(BF16)


def f64(x):
    return np.asarray(x).astype(np.float64)


N, M0, D0, M1, D1, M2, D2 = 1536, 512, 1, 512, 3, 256, 5
IRREPS = [(M0, D0), (M1, D1), (M2, D2)]
IN_DIM = sum(m * d for m, d in IRREPS)


def setup_inputs():
    s0, s1 = mx_kscale(M0), mx_kscale(M1)
    sx = np.concatenate([np.repeat(s0, D0), np.repeat(s1, D1), np.ones(M2 * D2)])
    return {"x": bf(np.random.standard_normal((N, IN_DIM)) * sx),
            "w0": bf(np.random.standard_normal((M0, M0)) * 0.4 / s0[:, None]),
            "w1": bf(np.random.standard_normal((M1, M1)) * 0.4 / s1[:, None]),
            "w2": bf(np.random.standard_normal((M2, M2)) * 0.4)}


def reference(x, w0, w1, w2):
    x = f64(x)
    outs = []
    off = 0
    for (mul, d), w, quantised in zip(IRREPS, [f64(w0), f64(w1), f64(w2)], [True, True, False]):
        blk = x[:, off:off + mul * d].reshape(N, mul, d)
        if quantised:
            y = mxq(blk, 1, "e4m3").transpose(0, 2, 1) @ mxq(w, 0, "e4m3")
        else:
            y = blk.transpose(0, 2, 1) @ w
        y = (1.0 / np.sqrt(mul)) * y.transpose(0, 2, 1)
        outs.append(y.reshape(N, mul * d))
        off += mul * d
    return np.concatenate(outs, axis=-1)

@@ -1,0 +1,216 @@
+from contextlib import ExitStack
+import math
+
+import concourse.mybir as mybir
+from concourse.masks import make_identity
+
+FP8X4 = mybir.dt.float8_e4m3fn_x4
+BF16 = mybir.dt.bfloat16
+F32 = mybir.dt.float32
+U32 = mybir.dt.uint32
+U8 = mybir.dt.uint8
+MULT = mybir.AluOpType.mult
+
+P = 128
+ROWS = 1536
+TILES = ROWS // P
+COLS = 3328
+WORDS = COLS // 2
+OFF1 = 512
+OFF2 = 2048
+S01 = 1.0 / math.sqrt(512.0)
+S2 = 1.0 / math.sqrt(256.0)
+LOAD_GROUPS = [1, 1, 2, 4, 4]
+W2_CHUNKS = [(0, 88), (88, 88), (176, 80)]
+
+FLOPS = 2 * ROWS * (512 * 512 * 4 + 256 * 256 * 5)
+
+
+def tile_linear_kernel(tc, x, w0, w1, w2, out):
+    nc = tc.nc
+    xf = x.rearrange("(p t) c -> p (t c)", t=TILES)
+    of = out.rearrange("(p t) c -> p (t c)", t=TILES)
+
+    def scaled(eng, dst, src, factor):
+        if eng == "v":
+            nc.vector.tensor_scalar(out=dst, in0=src, scalar1=factor, scalar2=None, op0=MULT)
+        else:
+            nc.scalar.mul(dst, src, factor)
+
+    def moved(eng, dst, src):
+        if eng == "v":
+            nc.vector.tensor_copy(out=dst, in_=src)
+        else:
+            nc.scalar.copy(dst, src)
+
+    with ExitStack() as ctx:
+        keep = ctx.enter_context(tc.tile_pool(name="keep", bufs=1))
+        stage = ctx.enter_context(tc.tile_pool(name="stage", bufs=3))
+        outs = ctx.enter_context(tc.tile_pool(name="outs", bufs=5))
+        psum = ctx.enter_context(tc.psum_pool(name="psum", bufs=8))
+
+        ident = keep.tile([P, P], F32, name="ident")
+        make_identity(nc, ident[:])
+
+        x_of_tile = []
+        x_groups = []
+        t0 = 0
+        for g, n in enumerate(LOAD_GROUPS):
+            xg = keep.tile([P, n * COLS], BF16, name="x%d" % g)
+            x_groups.append((xg, t0, n))
+            for k in range(n):
+                x_of_tile.append((xg, k))
+            t0 += n
+
+        def load_group(g):
+            xg, first, n = x_groups[g]
+            nc.sync.dma_start(out=xg[:], in_=xf[:, first * COLS:(first + n) * COLS])
+
+        w_raw = []
+        load_group(0)
+        for name, w in (("w1", w1), ("w0", w0)):
+            raw = keep.tile([P, 4, 512], BF16, name="raw_" + name)
+            nc.sync.dma_start(
+                out=raw[:].rearrange("p (h e) c -> p h (e c)", h=2),
+                in_=w.rearrange("(h p e) c -> p h (e c)", h=2, e=2),
+            )
+            w_raw.append(raw)
+        w2_sb = keep.tile([P, 2, 256], BF16, name="w2_sb")
+        nc.sync.dma_start(out=w2_sb[:], in_=w2.rearrange("(m e) c -> m e c", e=2))
+        for g in range(1, len(LOAD_GROUPS)):
+            load_group(g)
+
+        w_codes = []
+        w_scales = []
+        for j, (name, eng) in enumerate((("w1", "v"), ("w0", "s"))):
+            grouped_w = keep.tile([P, 512, 4], BF16, name="grp_" + name, align_bytes=64)
+            moved(eng, grouped_w[:], w_raw[j][:].rearrange("p t c -> p c t"))
+            codes = keep.tile([P, 512], U32, name="codes_" + name, align_bytes=64)
+            scales = keep.tile([P, 512], U8, name="scales_" + name, align_bytes=64)
+            w_codes.append((grouped_w, codes, scales))
+
+        def quantise_weights(j):
+            grouped_w, codes, scales = w_codes[j]
+            nc.vector.quantize_mx(
+                out=codes[:].bitcast(FP8X4),
+                scales=scales[:],
+                in_=grouped_w[:].rearrange("p c t -> p (c t)"),
+            )
+
+        state = {}
+
+        def front(t):
+            xg, k = x_of_tile[t]
+            xb = xg[:, k * COLS:(k + 1) * COLS]
+            xw = xg[:].bitcast(F32)[:, k * WORDS:(k + 1) * WORDS]
+            xs1 = stage.tile([P, 3 * 512], BF16, name="xs1")
+            nc.vector.tensor_copy(
+                out=xs1[:].rearrange("p (i u) -> p i u", i=3),
+                in_=xb[:, OFF1:OFF2].rearrange("p (u i) -> p i u", i=3),
+            )
+            xs1w = xs1[:].bitcast(F32)
+            xT2 = stage.tile([P, 10 * P], BF16, name="xT2")
+            tb2 = psum.tile([P, 512], F32, name="tb2", tag="bank")
+            for r in range(4):
+                nc.tensor.transpose(
+                    tb2[:, r * P:(r + 1) * P],
+                    xw[:, OFF2 // 2 + r:WORDS:5],
+                    ident[:],
+                )
+            tb3 = psum.tile([P, 512], F32, name="tb3", tag="bank")
+            nc.tensor.transpose(tb3[:, 0:P], xw[:, OFF2 // 2 + 4:WORDS:5], ident[:])
+            moved(
+                "s",
+                xT2[:, 0:8 * P].rearrange("p (r e n) -> p r e n", r=4, e=2),
+                tb2[:].bitcast(BF16).rearrange("p (r n e) -> p r e n", r=4, e=2),
+            )
+            moved(
+                "s",
+                xT2[:, 8 * P:10 * P].rearrange("p (e n) -> p e n", e=2),
+                tb3[:].bitcast(BF16)[:, 0:2 * P].rearrange("p (n e) -> p e n", e=2),
+            )
+            grouped = stage.tile([P, 4 * P * 4], BF16, name="grouped", align_bytes=64)
+            gw = grouped[:].bitcast(F32)
+            for b in range(2):
+                tb = psum.tile([P, 512], F32, name="tb01", tag="bank")
+                for s2 in range(2):
+                    slot = 2 * b + s2
+                    for h in range(2):
+                        if slot == 0:
+                            src = xw[:, h * P:(h + 1) * P]
+                        else:
+                            base = (slot - 1) * 256 + h * P
+                            src = xs1w[:, base:base + P]
+                        q = 2 * s2 + h
+                        nc.tensor.transpose(tb[:, q * P:(q + 1) * P], src, ident[:])
+                moved(
+                    "v",
+                    gw[:, b * 512:(b + 1) * 512].rearrange("p (s n h) -> p s n h", s=2, h=2),
+                    tb[:].rearrange("p (s h n) -> p s n h", s=2, h=2),
+                )
+            codes = stage.tile([P, 512], U32, name="codes", align_bytes=64)
+            scales = stage.tile([P, 512], U8, name="scales", align_bytes=64)
+            nc.vector.quantize_mx(out=codes[:].bitcast(FP8X4), scales=scales[:], in_=grouped[:])
+            state[t] = (codes, scales, xT2)
+
+        def back(t):
+            codes, scales, xT2 = state[t]
+            o = outs.tile([P, COLS], F32, name="o")
+            c1, s1 = w_codes[0][1], w_codes[0][2]
+            c0, s0 = w_codes[1][1], w_codes[1][2]
+            for c in range(4):
+                acc = psum.tile([P, 512], F32, name="acc1", tag="bank")
+                for i in range(3):
+                    nc.tensor.matmul_mx(
+                        out=acc[:, i * P:(i + 1) * P],
+                        lhsT=codes[:, (i + 1) * P:(i + 2) * P].bitcast(FP8X4),
+                        lhsT_scale=scales[:, (i + 1) * P:(i + 2) * P],
+                        rhs=c1[:, c * P:(c + 1) * P].bitcast(FP8X4),
+                        rhs_scale=s1[:, c * P:(c + 1) * P],
+                        start=True,
+                        stop=True,
+                    )
+                scaled(
+                    "v" if c == 1 else "s",
+                    o[:, OFF1 + c * 384:OFF1 + (c + 1) * 384].rearrange("p (w i) -> p w i", i=3),
+                    acc[:, 0:384].rearrange("p (i w) -> p w i", i=3),
+                    S01,
+                )
+            acc0 = psum.tile([P, 512], F32, name="acc0", tag="bank")
+            nc.tensor.matmul_mx(
+                out=acc0[:],
+                lhsT=codes[:, 0:P].bitcast(FP8X4),
+                lhsT_scale=scales[:, 0:P],
+                rhs=c0[:].bitcast(FP8X4),
+                rhs_scale=s0[:],
+                start=True,
+                stop=True,
+            )
+            scaled("v", o[:, 0:OFF1], acc0[:], S01)
+            for ci, (wlo, wn) in enumerate(W2_CHUNKS):
+                acc2 = psum.tile([P, 512], F32, name="acc2", tag="bank")
+                for i in range(5):
+                    for e in range(2):
+                        f = 5 * e + i
+                        nc.tensor.matmul(
+                            out=acc2[:, i * wn:(i + 1) * wn],
+                            lhsT=xT2[:, f * P:(f + 1) * P],
+                            rhs=w2_sb[:, e, wlo:wlo + wn],
+                            start=(e == 0),
+                            stop=(e == 1),
+                        )
+                scaled(
+                    "v" if ci == 1 else "s",
+                    o[:, OFF2 + 5 * wlo:OFF2 + 5 * (wlo + wn)].rearrange("p (w i) -> p w i", i=5),
+                    acc2[:, 0:5 * wn].rearrange("p (i w) -> p w i", i=5),
+                    S2,
+                )
+            nc.sync.dma_start(out=of[:, t * COLS:(t + 1) * COLS], in_=o[:])
+
+        front(0)
+        quantise_weights(0)
+        quantise_weights(1)
+        for t in range(TILES):
+            if t + 1 < TILES:
+                front(t + 1)
+            back(t)

@@ -10,6 +10,7 @@ F32 = mybir.dt.float32
 U32 = mybir.dt.uint32
 U8 = mybir.dt.uint8
 MULT = mybir.AluOpType.mult
+ADD = mybir.AluOpType.add
 
 P = 128
 ROWS = 1536
@@ -104,10 +105,14 @@ def tile_linear_kernel(tc, x, w0, w1, w2, out):
             xb = xg[:, k * COLS:(k + 1) * COLS]
             xw = xg[:].bitcast(F32)[:, k * WORDS:(k + 1) * WORDS]
             xs1 = stage.tile([P, 3 * 512], BF16, name="xs1")
-            nc.vector.tensor_copy(
-                out=xs1[:].rearrange("p (i u) -> p i u", i=3),
-                in_=xb[:, OFF1:OFF2].rearrange("p (u i) -> p i u", i=3),
-            )
+            xs1_dst = xs1[:].rearrange("p (i u) -> p i u", i=3)
+            xs1_src = xb[:, OFF1:OFF2].rearrange("p (u i) -> p i u", i=3)
+            if t == 0:
+                nc.vector.tensor_copy(out=xs1_dst, in_=xs1_src)
+            else:
+                nc.gpsimd.tensor_scalar(
+                    out=xs1_dst, in0=xs1_src, scalar1=1.0, scalar2=0.0, op0=MULT, op1=ADD
+                )
             xs1w = xs1[:].bitcast(F32)
             xT2 = stage.tile([P, 10 * P], BF16, name="xT2")
             tb2 = psum.tile([P, 512], F32, name="tb2", tag="bank")
@@ -125,7 +130,7 @@ def tile_linear_kernel(tc, x, w0, w1, w2, out):
                 tb2[:].bitcast(BF16).rearrange("p (r n e) -> p r e n", r=4, e=2),
             )
             moved(
-                "s",
+                "v",
                 xT2[:, 8 * P:10 * P].rearrange("p (e n) -> p e n", e=2),
                 tb3[:].bitcast(BF16)[:, 0:2 * P].rearrange("p (n e) -> p e n", e=2),
             )

@@ -49,6 +49,7 @@ def tile_linear_kernel(tc, x, w0, w1, w2, out):
         stage = ctx.enter_context(tc.tile_pool(name="stage", bufs=3))
         outs = ctx.enter_context(tc.tile_pool(name="outs", bufs=5))
         psum = ctx.enter_context(tc.psum_pool(name="psum", bufs=8))
+        ctx.enter_context(tc.manual_schedule())
 
         ident = keep.tile([P, P], F32, name="ident")
         make_identity(nc, ident[:])
@@ -83,12 +84,14 @@ def tile_linear_kernel(tc, x, w0, w1, w2, out):
 
         w_codes = []
         w_scales = []
-        for j, (name, eng) in enumerate((("w1", "v"), ("w0", "s"))):
+        for name in ("w1", "w0"):
             grouped_w = keep.tile([P, 512, 4], BF16, name="grp_" + name, align_bytes=64)
-            moved(eng, grouped_w[:], w_raw[j][:].rearrange("p t c -> p c t"))
             codes = keep.tile([P, 512], U32, name="codes_" + name, align_bytes=64)
             scales = keep.tile([P, 512], U8, name="scales_" + name, align_bytes=64)
             w_codes.append((grouped_w, codes, scales))
+
+        def regroup_weights(j, eng):
+            moved(eng, w_codes[j][0][:], w_raw[j][:].rearrange("p t c -> p c t"))
 
         def quantise_weights(j):
             grouped_w, codes, scales = w_codes[j]
@@ -100,11 +103,13 @@ def tile_linear_kernel(tc, x, w0, w1, w2, out):
 
         state = {}
 
-        def front(t):
+        sorted1 = {}
+
+        def presort(t):
             xg, k = x_of_tile[t]
             xb = xg[:, k * COLS:(k + 1) * COLS]
-            xw = xg[:].bitcast(F32)[:, k * WORDS:(k + 1) * WORDS]
             xs1 = stage.tile([P, 3 * 512], BF16, name="xs1")
+            sorted1[t] = xs1
             xs1_dst = xs1[:].rearrange("p (i u) -> p i u", i=3)
             xs1_src = xb[:, OFF1:OFF2].rearrange("p (u i) -> p i u", i=3)
             if t == 0:
@@ -113,7 +118,11 @@ def tile_linear_kernel(tc, x, w0, w1, w2, out):
                 nc.gpsimd.tensor_scalar(
                     out=xs1_dst, in0=xs1_src, scalar1=1.0, scalar2=0.0, op0=MULT, op1=ADD
                 )
-            xs1w = xs1[:].bitcast(F32)
+
+        def transposes(t):
+            xg, k = x_of_tile[t]
+            xw = xg[:].bitcast(F32)[:, k * WORDS:(k + 1) * WORDS]
+            xs1w = sorted1[t][:].bitcast(F32)
             xT2 = stage.tile([P, 10 * P], BF16, name="xT2")
             tb2 = psum.tile([P, 512], F32, name="tb2", tag="bank")
             for r in range(4):
@@ -155,11 +164,14 @@ def tile_linear_kernel(tc, x, w0, w1, w2, out):
                 )
             codes = stage.tile([P, 512], U32, name="codes", align_bytes=64)
             scales = stage.tile([P, 512], U8, name="scales", align_bytes=64)
+            state[t] = (codes, scales, xT2, grouped)
+
+        def quantise(t):
+            codes, scales, xT2, grouped = state[t]
             nc.vector.quantize_mx(out=codes[:].bitcast(FP8X4), scales=scales[:], in_=grouped[:])
-            state[t] = (codes, scales, xT2)
 
         def back(t):
-            codes, scales, xT2 = state[t]
+            codes, scales, xT2, grouped = state[t]
             o = outs.tile([P, COLS], F32, name="o")
             c1, s1 = w_codes[0][1], w_codes[0][2]
             c0, s0 = w_codes[1][1], w_codes[1][2]
@@ -181,6 +193,8 @@ def tile_linear_kernel(tc, x, w0, w1, w2, out):
                     acc[:, 0:384].rearrange("p (i w) -> p w i", i=3),
                     S01,
                 )
+                if c == 1 and t + 1 < TILES:
+                    quantise(t + 1)
             acc0 = psum.tile([P, 512], F32, name="acc0", tag="bank")
             nc.tensor.matmul_mx(
                 out=acc0[:],
@@ -212,10 +226,15 @@ def tile_linear_kernel(tc, x, w0, w1, w2, out):
                 )
             nc.sync.dma_start(out=of[:, t * COLS:(t + 1) * COLS], in_=o[:])
 
-        front(0)
+        presort(0)
+        regroup_weights(0, "v")
+        transposes(0)
+        regroup_weights(1, "s")
         quantise_weights(0)
+        quantise(0)
         quantise_weights(1)
         for t in range(TILES):
             if t + 1 < TILES:
-                front(t + 1)
+                presort(t + 1)
+                transposes(t + 1)
             back(t)

@@ -21,8 +21,10 @@ OFF1 = 512
 OFF2 = 2048
 S01 = 1.0 / math.sqrt(512.0)
 S2 = 1.0 / math.sqrt(256.0)
-LOAD_GROUPS = [1, 1, 2, 4, 4]
+LOAD_GROUPS = [(1, 1), (2, 1), (3, 1), (4, 4), (8, 4)]
 W2_CHUNKS = [(0, 88), (88, 88), (176, 80)]
+WHOLE = [(0, COLS)]
+TAIL_PIECES = [(OFF2, COLS), (0, 1280), (1280, OFF2)]
 
 FLOPS = 2 * ROWS * (512 * 512 * 4 + 256 * 256 * 5)
 
@@ -41,8 +43,10 @@ def tile_linear_kernel(tc, x, w0, w1, w2, out):
     def moved(eng, dst, src):
         if eng == "v":
             nc.vector.tensor_copy(out=dst, in_=src)
-        else:
+        elif eng == "s":
             nc.scalar.copy(dst, src)
+        else:
+            nc.gpsimd.tensor_scalar(out=dst, in0=src, scalar1=1.0, scalar2=0.0, op0=MULT, op1=ADD)
 
     with ExitStack() as ctx:
         keep = ctx.enter_context(tc.tile_pool(name="keep", bufs=1))
@@ -54,85 +58,80 @@ def tile_linear_kernel(tc, x, w0, w1, w2, out):
         ident = keep.tile([P, P], F32, name="ident")
         make_identity(nc, ident[:])
 
-        x_of_tile = []
-        x_groups = []
-        t0 = 0
-        for g, n in enumerate(LOAD_GROUPS):
-            xg = keep.tile([P, n * COLS], BF16, name="x%d" % g)
-            x_groups.append((xg, t0, n))
-            for k in range(n):
-                x_of_tile.append((xg, k))
-            t0 += n
-
-        def load_group(g):
-            xg, first, n = x_groups[g]
-            nc.sync.dma_start(out=xg[:], in_=xf[:, first * COLS:(first + n) * COLS])
-
-        w_raw = []
-        load_group(0)
-        for name, w in (("w1", w1), ("w0", w0)):
+        def load_weight(name, w):
             raw = keep.tile([P, 4, 512], BF16, name="raw_" + name)
             nc.sync.dma_start(
                 out=raw[:].rearrange("p (h e) c -> p h (e c)", h=2),
                 in_=w.rearrange("(h p e) c -> p h (e c)", h=2, e=2),
             )
-            w_raw.append(raw)
+            return raw
+
+        x_block1 = {}
+        x_words01 = {}
+        x_words2 = {}
+        x0a = keep.tile([P, OFF2], BF16, name="x0a")
+        nc.sync.dma_start(out=x0a[:], in_=xf[:, 0:OFF2])
+        raw1 = load_weight("w1", w1)
+        x0b = keep.tile([P, COLS - OFF2], BF16, name="x0b")
+        nc.sync.dma_start(out=x0b[:], in_=xf[:, OFF2:COLS])
         w2_sb = keep.tile([P, 2, 256], BF16, name="w2_sb")
         nc.sync.dma_start(out=w2_sb[:], in_=w2.rearrange("(m e) c -> m e c", e=2))
-        for g in range(1, len(LOAD_GROUPS)):
-            load_group(g)
+        raw0 = load_weight("w0", w0)
+        x_block1[0] = x0a[:, OFF1:OFF2]
+        x_words01[0] = x0a[:].bitcast(F32)
+        x_words2[0] = x0b[:].bitcast(F32)
+        for first, n in LOAD_GROUPS:
+            xg = keep.tile([P, n * COLS], BF16, name="x%d" % first)
+            nc.sync.dma_start(out=xg[:], in_=xf[:, first * COLS:(first + n) * COLS])
+            xgw = xg[:].bitcast(F32)
+            for k in range(n):
+                x_block1[first + k] = xg[:, k * COLS + OFF1:k * COLS + OFF2]
+                x_words01[first + k] = xgw[:, k * WORDS:k * WORDS + OFF2 // 2]
+                x_words2[first + k] = xgw[:, k * WORDS + OFF2 // 2:(k + 1) * WORDS]
 
-        w_codes = []
-        w_scales = []
-        for name in ("w1", "w0"):
+        def weight_tiles(name):
             grouped_w = keep.tile([P, 512, 4], BF16, name="grp_" + name, align_bytes=64)
             codes = keep.tile([P, 512], U32, name="codes_" + name, align_bytes=64)
             scales = keep.tile([P, 512], U8, name="scales_" + name, align_bytes=64)
-            w_codes.append((grouped_w, codes, scales))
+            return grouped_w, codes, scales
 
-        def regroup_weights(j, eng):
-            moved(eng, w_codes[j][0][:], w_raw[j][:].rearrange("p t c -> p c t"))
+        grp1, c1, s1 = weight_tiles("w1")
+        grp0, c0, s0 = weight_tiles("w0")
 
-        def quantise_weights(j):
-            grouped_w, codes, scales = w_codes[j]
+        def regroup(eng, grouped_w, raw, half):
+            cols = slice(256 * half, 256 * (half + 1))
+            moved(eng, grouped_w[:, cols, :], raw[:, :, cols].rearrange("p t c -> p c t"))
+
+        def quantise_weight(grouped_w, codes, scales):
             nc.vector.quantize_mx(
                 out=codes[:].bitcast(FP8X4),
                 scales=scales[:],
                 in_=grouped_w[:].rearrange("p c t -> p (c t)"),
             )
 
-        state = {}
-
         sorted1 = {}
+        mx_in = {}
+        plain_in = {}
+        out_pieces = {}
 
-        def presort(t):
-            xg, k = x_of_tile[t]
-            xb = xg[:, k * COLS:(k + 1) * COLS]
+        def presort(t, eng):
             xs1 = stage.tile([P, 3 * 512], BF16, name="xs1")
             sorted1[t] = xs1
-            xs1_dst = xs1[:].rearrange("p (i u) -> p i u", i=3)
-            xs1_src = xb[:, OFF1:OFF2].rearrange("p (u i) -> p i u", i=3)
-            if t == 0:
-                nc.vector.tensor_copy(out=xs1_dst, in_=xs1_src)
-            else:
-                nc.gpsimd.tensor_scalar(
-                    out=xs1_dst, in0=xs1_src, scalar1=1.0, scalar2=0.0, op0=MULT, op1=ADD
-                )
+            moved(
+                eng,
+                xs1[:].rearrange("p (i u) -> p i u", i=3),
+                x_block1[t].rearrange("p (u i) -> p i u", i=3),
+            )
 
-        def transposes(t):
-            xg, k = x_of_tile[t]
-            xw = xg[:].bitcast(F32)[:, k * WORDS:(k + 1) * WORDS]
-            xs1w = sorted1[t][:].bitcast(F32)
+        def transpose2(t):
+            xw = x_words2[t]
             xT2 = stage.tile([P, 10 * P], BF16, name="xT2")
+            plain_in[t] = xT2
             tb2 = psum.tile([P, 512], F32, name="tb2", tag="bank")
             for r in range(4):
-                nc.tensor.transpose(
-                    tb2[:, r * P:(r + 1) * P],
-                    xw[:, OFF2 // 2 + r:WORDS:5],
-                    ident[:],
-                )
+                nc.tensor.transpose(tb2[:, r * P:(r + 1) * P], xw[:, r:640:5], ident[:])
             tb3 = psum.tile([P, 512], F32, name="tb3", tag="bank")
-            nc.tensor.transpose(tb3[:, 0:P], xw[:, OFF2 // 2 + 4:WORDS:5], ident[:])
+            nc.tensor.transpose(tb3[:, 0:P], xw[:, 4:640:5], ident[:])
             moved(
                 "s",
                 xT2[:, 0:8 * P].rearrange("p (r e n) -> p r e n", r=4, e=2),
@@ -143,6 +142,10 @@ def tile_linear_kernel(tc, x, w0, w1, w2, out):
                 xT2[:, 8 * P:10 * P].rearrange("p (e n) -> p e n", e=2),
                 tb3[:].bitcast(BF16)[:, 0:2 * P].rearrange("p (n e) -> p e n", e=2),
             )
+
+        def transpose01(t):
+            xw = x_words01[t]
+            xs1w = sorted1[t][:].bitcast(F32)
             grouped = stage.tile([P, 4 * P * 4], BF16, name="grouped", align_bytes=64)
             gw = grouped[:].bitcast(F32)
             for b in range(2):
@@ -164,37 +167,52 @@ def tile_linear_kernel(tc, x, w0, w1, w2, out):
                 )
             codes = stage.tile([P, 512], U32, name="codes", align_bytes=64)
             scales = stage.tile([P, 512], U8, name="scales", align_bytes=64)
-            state[t] = (codes, scales, xT2, grouped)
+            mx_in[t] = (codes, scales, grouped)
 
         def quantise(t):
-            codes, scales, xT2, grouped = state[t]
+            codes, scales, grouped = mx_in[t]
             nc.vector.quantize_mx(out=codes[:].bitcast(FP8X4), scales=scales[:], in_=grouped[:])
 
-        def back(t):
-            codes, scales, xT2, grouped = state[t]
-            o = outs.tile([P, COLS], F32, name="o")
-            c1, s1 = w_codes[0][1], w_codes[0][2]
-            c0, s0 = w_codes[1][1], w_codes[1][2]
-            for c in range(4):
-                acc = psum.tile([P, 512], F32, name="acc1", tag="bank")
-                for i in range(3):
-                    nc.tensor.matmul_mx(
-                        out=acc[:, i * P:(i + 1) * P],
-                        lhsT=codes[:, (i + 1) * P:(i + 2) * P].bitcast(FP8X4),
-                        lhsT_scale=scales[:, (i + 1) * P:(i + 2) * P],
-                        rhs=c1[:, c * P:(c + 1) * P].bitcast(FP8X4),
-                        rhs_scale=s1[:, c * P:(c + 1) * P],
-                        start=True,
-                        stop=True,
-                    )
-                scaled(
-                    "v" if c == 1 else "s",
-                    o[:, OFF1 + c * 384:OFF1 + (c + 1) * 384].rearrange("p (w i) -> p w i", i=3),
-                    acc[:, 0:384].rearrange("p (i w) -> p w i", i=3),
-                    S01,
+        def open_out(t):
+            pieces = []
+            for lo, hi in (TAIL_PIECES if t == TILES - 1 else WHOLE):
+                piece = outs.tile(
+                    [P, hi - lo], F32, name="o%d" % lo, bufs=(1 if t == TILES - 1 else 5),
+                    tag=("tail%d" % lo if t == TILES - 1 else "o"),
                 )
-                if c == 1 and t + 1 < TILES:
-                    quantise(t + 1)
+                pieces.append((lo, hi, piece))
+            out_pieces[t] = pieces
+
+        def dst(t, lo, hi):
+            hits = [piece[:, lo - a:hi - a] for a, b, piece in out_pieces[t] if a <= lo and hi <= b]
+            return hits[0]
+
+        def store(t, k):
+            lo, hi, piece = out_pieces[t][k]
+            nc.sync.dma_start(out=of[:, t * COLS + lo:t * COLS + hi], in_=piece[:])
+
+        def mx1(t, c, eng):
+            codes, scales, grouped = mx_in[t]
+            acc = psum.tile([P, 512], F32, name="acc1", tag="bank")
+            for i in range(3):
+                nc.tensor.matmul_mx(
+                    out=acc[:, i * P:(i + 1) * P],
+                    lhsT=codes[:, (i + 1) * P:(i + 2) * P].bitcast(FP8X4),
+                    lhsT_scale=scales[:, (i + 1) * P:(i + 2) * P],
+                    rhs=c1[:, c * P:(c + 1) * P].bitcast(FP8X4),
+                    rhs_scale=s1[:, c * P:(c + 1) * P],
+                    start=True,
+                    stop=True,
+                )
+            scaled(
+                eng,
+                dst(t, OFF1 + c * 384, OFF1 + (c + 1) * 384).rearrange("p (w i) -> p w i", i=3),
+                acc[:, 0:384].rearrange("p (i w) -> p w i", i=3),
+                S01,
+            )
+
+        def mx0(t, eng):
+            codes, scales, grouped = mx_in[t]
             acc0 = psum.tile([P, 512], F32, name="acc0", tag="bank")
             nc.tensor.matmul_mx(
                 out=acc0[:],
@@ -205,36 +223,73 @@ def tile_linear_kernel(tc, x, w0, w1, w2, out):
                 start=True,
                 stop=True,
             )
-            scaled("v", o[:, 0:OFF1], acc0[:], S01)
-            for ci, (wlo, wn) in enumerate(W2_CHUNKS):
-                acc2 = psum.tile([P, 512], F32, name="acc2", tag="bank")
-                for i in range(5):
-                    for e in range(2):
-                        f = 5 * e + i
-                        nc.tensor.matmul(
-                            out=acc2[:, i * wn:(i + 1) * wn],
-                            lhsT=xT2[:, f * P:(f + 1) * P],
-                            rhs=w2_sb[:, e, wlo:wlo + wn],
-                            start=(e == 0),
-                            stop=(e == 1),
-                        )
-                scaled(
-                    "v" if ci == 1 else "s",
-                    o[:, OFF2 + 5 * wlo:OFF2 + 5 * (wlo + wn)].rearrange("p (w i) -> p w i", i=5),
-                    acc2[:, 0:5 * wn].rearrange("p (i w) -> p w i", i=5),
-                    S2,
-                )
-            nc.sync.dma_start(out=of[:, t * COLS:(t + 1) * COLS], in_=o[:])
+            scaled(eng, dst(t, 0, OFF1), acc0[:], S01)
 
-        presort(0)
-        regroup_weights(0, "v")
-        transposes(0)
-        regroup_weights(1, "s")
-        quantise_weights(0)
+        def plain(t, ci, eng):
+            xT2 = plain_in[t]
+            wlo, wn = W2_CHUNKS[ci]
+            acc2 = psum.tile([P, 512], F32, name="acc2", tag="bank")
+            for i in range(5):
+                for e in range(2):
+                    f = 5 * e + i
+                    nc.tensor.matmul(
+                        out=acc2[:, i * wn:(i + 1) * wn],
+                        lhsT=xT2[:, f * P:(f + 1) * P],
+                        rhs=w2_sb[:, e, wlo:wlo + wn],
+                        start=(e == 0),
+                        stop=(e == 1),
+                    )
+            scaled(
+                eng,
+                dst(t, OFF2 + 5 * wlo, OFF2 + 5 * (wlo + wn)).rearrange("p (w i) -> p w i", i=5),
+                acc2[:, 0:5 * wn].rearrange("p (i w) -> p w i", i=5),
+                S2,
+            )
+
+        presort(0, "v")
+        regroup("v", grp1, raw1, 0)
+        regroup("s", grp1, raw1, 1)
+        transpose01(0)
+        quantise_weight(grp1, c1, s1)
         quantise(0)
-        quantise_weights(1)
-        for t in range(TILES):
-            if t + 1 < TILES:
-                presort(t + 1)
-                transposes(t + 1)
-            back(t)
+        transpose2(0)
+        regroup("g", grp0, raw0, 0)
+        regroup("s", grp0, raw0, 1)
+        open_out(0)
+        mx1(0, 0, "s")
+        mx1(0, 1, "v")
+        quantise_weight(grp0, c0, s0)
+        mx1(0, 2, "s")
+        mx1(0, 3, "v")
+        plain(0, 0, "s")
+        plain(0, 1, "v")
+        plain(0, 2, "s")
+        mx0(0, "v")
+        store(0, 0)
+        presort(1, "g")
+        transpose2(1)
+        transpose01(1)
+        for t in range(1, TILES):
+            last = t == TILES - 1
+            if not last:
+                presort(t + 1, "g")
+                transpose2(t + 1)
+                if t == 1:
+                    quantise(1)
+                transpose01(t + 1)
+            open_out(t)
+            plain(t, 0, "s")
+            plain(t, 1, "v")
+            if not last:
+                quantise(t + 1)
+            plain(t, 2, "s")
+            if last:
+                store(t, 0)
+            mx0(t, "v")
+            mx1(t, 0, "s")
+            mx1(t, 1, "v" if last else "s")
+            if last:
+                store(t, 1)
+            mx1(t, 2, "s" if last else "v")
+            mx1(t, 3, "v" if last else "s")
+            store(t, 2 if last else 0)

@@ -16,37 +16,37 @@ P = 128
 ROWS = 1536
 TILES = ROWS // P
 COLS = 3328
-WORDS = COLS // 2
+MUL01 = 512
+D1 = 3
 OFF1 = 512
+MUL2 = 256
+D2 = 5
 OFF2 = 2048
-S01 = 1.0 / math.sqrt(512.0)
-S2 = 1.0 / math.sqrt(256.0)
-LOAD_GROUPS = [(1, 1), (2, 1), (3, 1), (4, 4), (8, 4)]
-W2_CHUNKS = [(0, 88), (88, 88), (176, 80)]
-WHOLE = [(0, COLS)]
-TAIL_PIECES = [(OFF2, COLS), (0, 1280), (1280, OFF2)]
+PAIRS = COLS // 2
+BANK = 512
+OPERANDS = 1 + D1
+SCALE01 = 1.0 / math.sqrt(MUL01)
+SCALE2 = 1.0 / math.sqrt(MUL2)
+LOAD_GROUPS = [1, 1, 2, 4, 4]
+CHUNKS2 = [(0, 88), (88, 88), (176, 80)]
+CHUNK1 = 128
 
-FLOPS = 2 * ROWS * (512 * 512 * 4 + 256 * 256 * 5)
+FLOPS = 2 * ROWS * (MUL01 * MUL01 * (1 + D1) + MUL2 * MUL2 * D2)
 
 
 def tile_linear_kernel(tc, x, w0, w1, w2, out):
     nc = tc.nc
-    xf = x.rearrange("(p t) c -> p (t c)", t=TILES)
-    of = out.rearrange("(p t) c -> p (t c)", t=TILES)
+    x_rows = x.rearrange("(p t) c -> p (t c)", t=TILES)
+    out_rows = out.rearrange("(p t) c -> p (t c)", t=TILES)
 
-    def scaled(eng, dst, src, factor):
-        if eng == "v":
-            nc.vector.tensor_scalar(out=dst, in0=src, scalar1=factor, scalar2=None, op0=MULT)
-        else:
-            nc.scalar.mul(dst, src, factor)
+    def vector_scaled(dst, src, factor):
+        nc.vector.tensor_scalar(out=dst, in0=src, scalar1=factor, scalar2=None, op0=MULT)
 
-    def moved(eng, dst, src):
-        if eng == "v":
-            nc.vector.tensor_copy(out=dst, in_=src)
-        elif eng == "s":
-            nc.scalar.copy(dst, src)
-        else:
-            nc.gpsimd.tensor_scalar(out=dst, in0=src, scalar1=1.0, scalar2=0.0, op0=MULT, op1=ADD)
+    def scalar_scaled(dst, src, factor):
+        nc.scalar.mul(dst, src, factor)
+
+    drain1 = [scalar_scaled, vector_scaled, scalar_scaled, scalar_scaled]
+    drain2 = [scalar_scaled, vector_scaled, scalar_scaled]
 
     with ExitStack() as ctx:
         keep = ctx.enter_context(tc.tile_pool(name="keep", bufs=1))
@@ -58,238 +58,170 @@ def tile_linear_kernel(tc, x, w0, w1, w2, out):
         ident = keep.tile([P, P], F32, name="ident")
         make_identity(nc, ident[:])
 
-        def load_weight(name, w):
-            raw = keep.tile([P, 4, 512], BF16, name="raw_" + name)
+        x_tiles = []
+        x_loads = []
+        first = 0
+        for g, count in enumerate(LOAD_GROUPS):
+            x_sb = keep.tile([P, count * COLS], BF16, name="x%d" % g)
+            x_loads.append((x_sb, first, count))
+            for k in range(count):
+                x_tiles.append((x_sb, k))
+            first += count
+
+        def load_x(g):
+            x_sb, start, count = x_loads[g]
+            nc.sync.dma_start(out=x_sb[:], in_=x_rows[:, start * COLS:(start + count) * COLS])
+
+        def load_mx_weight(name, w):
+            raw = keep.tile([P, 4, MUL01], BF16, name="raw_" + name)
             nc.sync.dma_start(
                 out=raw[:].rearrange("p (h e) c -> p h (e c)", h=2),
                 in_=w.rearrange("(h p e) c -> p h (e c)", h=2, e=2),
             )
             return raw
 
-        x_block1 = {}
-        x_words01 = {}
-        x_words2 = {}
-        x0a = keep.tile([P, OFF2], BF16, name="x0a")
-        nc.sync.dma_start(out=x0a[:], in_=xf[:, 0:OFF2])
-        raw1 = load_weight("w1", w1)
-        x0b = keep.tile([P, COLS - OFF2], BF16, name="x0b")
-        nc.sync.dma_start(out=x0b[:], in_=xf[:, OFF2:COLS])
-        w2_sb = keep.tile([P, 2, 256], BF16, name="w2_sb")
+        load_x(0)
+        raw1 = load_mx_weight("w1", w1)
+        raw0 = load_mx_weight("w0", w0)
+        w2_sb = keep.tile([P, 2, MUL2], BF16, name="w2_sb")
         nc.sync.dma_start(out=w2_sb[:], in_=w2.rearrange("(m e) c -> m e c", e=2))
-        raw0 = load_weight("w0", w0)
-        x_block1[0] = x0a[:, OFF1:OFF2]
-        x_words01[0] = x0a[:].bitcast(F32)
-        x_words2[0] = x0b[:].bitcast(F32)
-        for first, n in LOAD_GROUPS:
-            xg = keep.tile([P, n * COLS], BF16, name="x%d" % first)
-            nc.sync.dma_start(out=xg[:], in_=xf[:, first * COLS:(first + n) * COLS])
-            xgw = xg[:].bitcast(F32)
-            for k in range(n):
-                x_block1[first + k] = xg[:, k * COLS + OFF1:k * COLS + OFF2]
-                x_words01[first + k] = xgw[:, k * WORDS:k * WORDS + OFF2 // 2]
-                x_words2[first + k] = xgw[:, k * WORDS + OFF2 // 2:(k + 1) * WORDS]
+        for g in range(1, len(LOAD_GROUPS)):
+            load_x(g)
 
-        def weight_tiles(name):
-            grouped_w = keep.tile([P, 512, 4], BF16, name="grp_" + name, align_bytes=64)
-            codes = keep.tile([P, 512], U32, name="codes_" + name, align_bytes=64)
-            scales = keep.tile([P, 512], U8, name="scales_" + name, align_bytes=64)
-            return grouped_w, codes, scales
+        def mx_weight_tiles(name):
+            grouped = keep.tile([P, MUL01, 4], BF16, name="grp_" + name, align_bytes=64)
+            codes = keep.tile([P, MUL01], U32, name="codes_" + name, align_bytes=64)
+            scales = keep.tile([P, MUL01], U8, name="scales_" + name, align_bytes=64)
+            return grouped, codes, scales
 
-        grp1, c1, s1 = weight_tiles("w1")
-        grp0, c0, s0 = weight_tiles("w0")
+        grouped1, codes1, scales1 = mx_weight_tiles("w1")
+        grouped0, codes0, scales0 = mx_weight_tiles("w0")
 
-        def regroup(eng, grouped_w, raw, half):
-            cols = slice(256 * half, 256 * (half + 1))
-            moved(eng, grouped_w[:, cols, :], raw[:, :, cols].rearrange("p t c -> p c t"))
-
-        def quantise_weight(grouped_w, codes, scales):
-            nc.vector.quantize_mx(
-                out=codes[:].bitcast(FP8X4),
-                scales=scales[:],
-                in_=grouped_w[:].rearrange("p c t -> p (c t)"),
-            )
+        def quantise(grouped_flat, codes, scales):
+            nc.vector.quantize_mx(out=codes[:].bitcast(FP8X4), scales=scales[:], in_=grouped_flat)
 
         sorted1 = {}
-        mx_in = {}
-        plain_in = {}
-        out_pieces = {}
+        mx_operands = {}
+        plain_operands = {}
 
-        def presort(t, eng):
-            xs1 = stage.tile([P, 3 * 512], BF16, name="xs1")
-            sorted1[t] = xs1
-            moved(
-                eng,
-                xs1[:].rearrange("p (i u) -> p i u", i=3),
-                x_block1[t].rearrange("p (u i) -> p i u", i=3),
+        def sort_block1(t):
+            x_sb, k = x_tiles[t]
+            by_component = stage.tile([P, D1 * MUL01], BF16, name="xs1")
+            sorted1[t] = by_component
+            nc.gpsimd.tensor_scalar(
+                out=by_component[:].rearrange("p (i u) -> p i u", i=D1),
+                in0=x_sb[:, k * COLS + OFF1:k * COLS + OFF2].rearrange("p (u i) -> p i u", i=D1),
+                scalar1=1.0,
+                scalar2=0.0,
+                op0=MULT,
+                op1=ADD,
             )
 
-        def transpose2(t):
-            xw = x_words2[t]
-            xT2 = stage.tile([P, 10 * P], BF16, name="xT2")
-            plain_in[t] = xT2
-            tb2 = psum.tile([P, 512], F32, name="tb2", tag="bank")
+        def transposes(t):
+            x_sb, k = x_tiles[t]
+            pairs = x_sb[:].bitcast(F32)[:, k * PAIRS:(k + 1) * PAIRS]
+            pairs1 = sorted1[t][:].bitcast(F32)
+
+            x2T = stage.tile([P, 2 * D2 * P], BF16, name="xT2")
+            plain_operands[t] = x2T
+            bank_a = psum.tile([P, BANK], F32, name="tb2", tag="bank")
             for r in range(4):
-                nc.tensor.transpose(tb2[:, r * P:(r + 1) * P], xw[:, r:640:5], ident[:])
-            tb3 = psum.tile([P, 512], F32, name="tb3", tag="bank")
-            nc.tensor.transpose(tb3[:, 0:P], xw[:, 4:640:5], ident[:])
-            moved(
-                "s",
-                xT2[:, 0:8 * P].rearrange("p (r e n) -> p r e n", r=4, e=2),
-                tb2[:].bitcast(BF16).rearrange("p (r n e) -> p r e n", r=4, e=2),
+                nc.tensor.transpose(bank_a[:, r * P:(r + 1) * P], pairs[:, OFF2 // 2 + r:PAIRS:D2], ident[:])
+            bank_b = psum.tile([P, BANK], F32, name="tb3", tag="bank")
+            nc.tensor.transpose(bank_b[:, 0:P], pairs[:, OFF2 // 2 + 4:PAIRS:D2], ident[:])
+            nc.scalar.copy(
+                x2T[:, 0:8 * P].rearrange("p (r e n) -> p r e n", r=4, e=2),
+                bank_a[:].bitcast(BF16).rearrange("p (r n e) -> p r e n", r=4, e=2),
             )
-            moved(
-                "v",
-                xT2[:, 8 * P:10 * P].rearrange("p (e n) -> p e n", e=2),
-                tb3[:].bitcast(BF16)[:, 0:2 * P].rearrange("p (n e) -> p e n", e=2),
+            nc.vector.tensor_copy(
+                out=x2T[:, 8 * P:10 * P].rearrange("p (e n) -> p e n", e=2),
+                in_=bank_b[:].bitcast(BF16)[:, 0:2 * P].rearrange("p (n e) -> p e n", e=2),
             )
 
-        def transpose01(t):
-            xw = x_words01[t]
-            xs1w = sorted1[t][:].bitcast(F32)
-            grouped = stage.tile([P, 4 * P * 4], BF16, name="grouped", align_bytes=64)
-            gw = grouped[:].bitcast(F32)
-            for b in range(2):
-                tb = psum.tile([P, 512], F32, name="tb01", tag="bank")
-                for s2 in range(2):
-                    slot = 2 * b + s2
+            grouped = stage.tile([P, OPERANDS * P * 4], BF16, name="grouped", align_bytes=64)
+            grouped_pairs = grouped[:].bitcast(F32)
+            for b in range(OPERANDS // 2):
+                bank = psum.tile([P, BANK], F32, name="tb01", tag="bank")
+                for s in (2 * b, 2 * b + 1):
                     for h in range(2):
-                        if slot == 0:
-                            src = xw[:, h * P:(h + 1) * P]
+                        if s == 0:
+                            src = pairs[:, h * P:(h + 1) * P]
                         else:
-                            base = (slot - 1) * 256 + h * P
-                            src = xs1w[:, base:base + P]
-                        q = 2 * s2 + h
-                        nc.tensor.transpose(tb[:, q * P:(q + 1) * P], src, ident[:])
-                moved(
-                    "v",
-                    gw[:, b * 512:(b + 1) * 512].rearrange("p (s n h) -> p s n h", s=2, h=2),
-                    tb[:].rearrange("p (s h n) -> p s n h", s=2, h=2),
+                            src = pairs1[:, (2 * (s - 1) + h) * P:(2 * (s - 1) + h + 1) * P]
+                        q = 2 * (s - 2 * b) + h
+                        nc.tensor.transpose(bank[:, q * P:(q + 1) * P], src, ident[:])
+                nc.vector.tensor_copy(
+                    out=grouped_pairs[:, b * BANK:(b + 1) * BANK].rearrange("p (s n h) -> p s n h", s=2, h=2),
+                    in_=bank[:].rearrange("p (s h n) -> p s n h", s=2, h=2),
                 )
-            codes = stage.tile([P, 512], U32, name="codes", align_bytes=64)
-            scales = stage.tile([P, 512], U8, name="scales", align_bytes=64)
-            mx_in[t] = (codes, scales, grouped)
+            codes = stage.tile([P, OPERANDS * P], U32, name="codes", align_bytes=64)
+            scales = stage.tile([P, OPERANDS * P], U8, name="scales", align_bytes=64)
+            mx_operands[t] = (grouped, codes, scales)
 
-        def quantise(t):
-            codes, scales, grouped = mx_in[t]
-            nc.vector.quantize_mx(out=codes[:].bitcast(FP8X4), scales=scales[:], in_=grouped[:])
+        def quantise_x(t):
+            grouped, codes, scales = mx_operands[t]
+            quantise(grouped[:], codes, scales)
 
-        def open_out(t):
-            pieces = []
-            for lo, hi in (TAIL_PIECES if t == TILES - 1 else WHOLE):
-                piece = outs.tile(
-                    [P, hi - lo], F32, name="o%d" % lo, bufs=(1 if t == TILES - 1 else 5),
-                    tag=("tail%d" % lo if t == TILES - 1 else "o"),
-                )
-                pieces.append((lo, hi, piece))
-            out_pieces[t] = pieces
+        def products(t):
+            grouped, codes, scales = mx_operands[t]
+            x2T = plain_operands[t]
+            o = outs.tile([P, COLS], F32, name="o")
 
-        def dst(t, lo, hi):
-            hits = [piece[:, lo - a:hi - a] for a, b, piece in out_pieces[t] if a <= lo and hi <= b]
-            return hits[0]
-
-        def store(t, k):
-            lo, hi, piece = out_pieces[t][k]
-            nc.sync.dma_start(out=of[:, t * COLS + lo:t * COLS + hi], in_=piece[:])
-
-        def mx1(t, c, eng):
-            codes, scales, grouped = mx_in[t]
-            acc = psum.tile([P, 512], F32, name="acc1", tag="bank")
-            for i in range(3):
+            def mx_pass(acc, s, w_codes, w_scales):
                 nc.tensor.matmul_mx(
-                    out=acc[:, i * P:(i + 1) * P],
-                    lhsT=codes[:, (i + 1) * P:(i + 2) * P].bitcast(FP8X4),
-                    lhsT_scale=scales[:, (i + 1) * P:(i + 2) * P],
-                    rhs=c1[:, c * P:(c + 1) * P].bitcast(FP8X4),
-                    rhs_scale=s1[:, c * P:(c + 1) * P],
+                    out=acc,
+                    lhsT=codes[:, s * P:(s + 1) * P].bitcast(FP8X4),
+                    lhsT_scale=scales[:, s * P:(s + 1) * P],
+                    rhs=w_codes.bitcast(FP8X4),
+                    rhs_scale=w_scales,
                     start=True,
                     stop=True,
                 )
-            scaled(
-                eng,
-                dst(t, OFF1 + c * 384, OFF1 + (c + 1) * 384).rearrange("p (w i) -> p w i", i=3),
-                acc[:, 0:384].rearrange("p (i w) -> p w i", i=3),
-                S01,
-            )
 
-        def mx0(t, eng):
-            codes, scales, grouped = mx_in[t]
-            acc0 = psum.tile([P, 512], F32, name="acc0", tag="bank")
-            nc.tensor.matmul_mx(
-                out=acc0[:],
-                lhsT=codes[:, 0:P].bitcast(FP8X4),
-                lhsT_scale=scales[:, 0:P],
-                rhs=c0[:].bitcast(FP8X4),
-                rhs_scale=s0[:],
-                start=True,
-                stop=True,
-            )
-            scaled(eng, dst(t, 0, OFF1), acc0[:], S01)
+            for c in range(MUL01 // CHUNK1):
+                cols = slice(c * CHUNK1, (c + 1) * CHUNK1)
+                acc1 = psum.tile([P, BANK], F32, name="acc1", tag="bank")
+                for i in range(D1):
+                    mx_pass(acc1[:, i * CHUNK1:(i + 1) * CHUNK1], 1 + i, codes1[:, cols], scales1[:, cols])
+                lo = OFF1 + c * D1 * CHUNK1
+                drain1[c](
+                    o[:, lo:lo + D1 * CHUNK1].rearrange("p (w i) -> p w i", i=D1),
+                    acc1[:, 0:D1 * CHUNK1].rearrange("p (i w) -> p w i", i=D1),
+                    SCALE01,
+                )
+                if c == 1 and t + 1 < TILES:
+                    quantise_x(t + 1)
+            acc0 = psum.tile([P, BANK], F32, name="acc0", tag="bank")
+            mx_pass(acc0[:], 0, codes0[:], scales0[:])
+            vector_scaled(o[:, 0:OFF1], acc0[:], SCALE01)
+            for c, (w_lo, w_n) in enumerate(CHUNKS2):
+                acc2 = psum.tile([P, BANK], F32, name="acc2", tag="bank")
+                for i in range(D2):
+                    for e2 in range(2):
+                        f = D2 * e2 + i
+                        nc.tensor.matmul(
+                            out=acc2[:, i * w_n:(i + 1) * w_n],
+                            lhsT=x2T[:, f * P:(f + 1) * P],
+                            rhs=w2_sb[:, e2, w_lo:w_lo + w_n],
+                            start=(e2 == 0),
+                            stop=(e2 == 1),
+                        )
+                drain2[c](
+                    o[:, OFF2 + D2 * w_lo:OFF2 + D2 * (w_lo + w_n)].rearrange("p (w i) -> p w i", i=D2),
+                    acc2[:, 0:D2 * w_n].rearrange("p (i w) -> p w i", i=D2),
+                    SCALE2,
+                )
+            nc.sync.dma_start(out=out_rows[:, t * COLS:(t + 1) * COLS], in_=o[:])
 
-        def plain(t, ci, eng):
-            xT2 = plain_in[t]
-            wlo, wn = W2_CHUNKS[ci]
-            acc2 = psum.tile([P, 512], F32, name="acc2", tag="bank")
-            for i in range(5):
-                for e in range(2):
-                    f = 5 * e + i
-                    nc.tensor.matmul(
-                        out=acc2[:, i * wn:(i + 1) * wn],
-                        lhsT=xT2[:, f * P:(f + 1) * P],
-                        rhs=w2_sb[:, e, wlo:wlo + wn],
-                        start=(e == 0),
-                        stop=(e == 1),
-                    )
-            scaled(
-                eng,
-                dst(t, OFF2 + 5 * wlo, OFF2 + 5 * (wlo + wn)).rearrange("p (w i) -> p w i", i=5),
-                acc2[:, 0:5 * wn].rearrange("p (i w) -> p w i", i=5),
-                S2,
-            )
-
-        presort(0, "v")
-        regroup("v", grp1, raw1, 0)
-        regroup("s", grp1, raw1, 1)
-        transpose01(0)
-        quantise_weight(grp1, c1, s1)
-        quantise(0)
-        transpose2(0)
-        regroup("g", grp0, raw0, 0)
-        regroup("s", grp0, raw0, 1)
-        open_out(0)
-        mx1(0, 0, "s")
-        mx1(0, 1, "v")
-        quantise_weight(grp0, c0, s0)
-        mx1(0, 2, "s")
-        mx1(0, 3, "v")
-        plain(0, 0, "s")
-        plain(0, 1, "v")
-        plain(0, 2, "s")
-        mx0(0, "v")
-        store(0, 0)
-        presort(1, "g")
-        transpose2(1)
-        transpose01(1)
-        for t in range(1, TILES):
-            last = t == TILES - 1
-            if not last:
-                presort(t + 1, "g")
-                transpose2(t + 1)
-                if t == 1:
-                    quantise(1)
-                transpose01(t + 1)
-            open_out(t)
-            plain(t, 0, "s")
-            plain(t, 1, "v")
-            if not last:
-                quantise(t + 1)
-            plain(t, 2, "s")
-            if last:
-                store(t, 0)
-            mx0(t, "v")
-            mx1(t, 0, "s")
-            mx1(t, 1, "v" if last else "s")
-            if last:
-                store(t, 1)
-            mx1(t, 2, "s" if last else "v")
-            mx1(t, 3, "v" if last else "s")
-            store(t, 2 if last else 0)
+        sort_block1(0)
+        nc.vector.tensor_copy(out=grouped1[:], in_=raw1[:].rearrange("p t c -> p c t"))
+        transposes(0)
+        nc.scalar.copy(grouped0[:], raw0[:].rearrange("p t c -> p c t"))
+        quantise(grouped1[:].rearrange("p c t -> p (c t)"), codes1, scales1)
+        quantise_x(0)
+        quantise(grouped0[:].rearrange("p c t -> p (c t)"), codes0, scales0)
+        for t in range(TILES):
+            if t + 1 < TILES:
+                sort_block1(t + 1)
+                transposes(t + 1)
+            products(t)

from contextlib import ExitStack
import math

import concourse.mybir as mybir
from concourse.masks import make_identity

FP8X4 = mybir.dt.float8_e4m3fn_x4
BF16 = mybir.dt.bfloat16
F32 = mybir.dt.float32
U32 = mybir.dt.uint32
U8 = mybir.dt.uint8
MULT = mybir.AluOpType.mult
ADD = mybir.AluOpType.add

P = 128
ROWS = 1536
TILES = ROWS // P
COLS = 3328
MUL01 = 512
D1 = 3
OFF1 = 512
MUL2 = 256
D2 = 5
OFF2 = 2048
PAIRS = COLS // 2
BANK = 512
OPERANDS = 1 + D1
SCALE01 = 1.0 / math.sqrt(MUL01)
SCALE2 = 1.0 / math.sqrt(MUL2)
LOAD_GROUPS = [1, 1, 2, 4, 4]
CHUNKS2 = [(0, 88), (88, 88), (176, 80)]
CHUNK1 = 128

FLOPS = 2 * ROWS * (MUL01 * MUL01 * (1 + D1) + MUL2 * MUL2 * D2)


def tile_linear_kernel(tc, x, w0, w1, w2, out):
    nc = tc.nc
    x_rows = x.rearrange("(p t) c -> p (t c)", t=TILES)
    out_rows = out.rearrange("(p t) c -> p (t c)", t=TILES)

    def vector_scaled(dst, src, factor):
        nc.vector.tensor_scalar(out=dst, in0=src, scalar1=factor, scalar2=None, op0=MULT)

    def scalar_scaled(dst, src, factor):
        nc.scalar.mul(dst, src, factor)

    drain1 = [scalar_scaled, vector_scaled, scalar_scaled, scalar_scaled]
    drain2 = [scalar_scaled, vector_scaled, scalar_scaled]

    with ExitStack() as ctx:
        keep = ctx.enter_context(tc.tile_pool(name="keep", bufs=1))
        stage = ctx.enter_context(tc.tile_pool(name="stage", bufs=3))
        outs = ctx.enter_context(tc.tile_pool(name="outs", bufs=5))
        psum = ctx.enter_context(tc.psum_pool(name="psum", bufs=8))
        ctx.enter_context(tc.manual_schedule())

        ident = keep.tile([P, P], F32, name="ident")
        make_identity(nc, ident[:])

        x_tiles = []
        x_loads = []
        first = 0
        for g, count in enumerate(LOAD_GROUPS):
            x_sb = keep.tile([P, count * COLS], BF16, name="x%d" % g)
            x_loads.append((x_sb, first, count))
            for k in range(count):
                x_tiles.append((x_sb, k))
            first += count

        def load_x(g):
            x_sb, start, count = x_loads[g]
            nc.sync.dma_start(out=x_sb[:], in_=x_rows[:, start * COLS:(start + count) * COLS])

        def load_mx_weight(name, w):
            raw = keep.tile([P, 4, MUL01], BF16, name="raw_" + name)
            nc.sync.dma_start(
                out=raw[:].rearrange("p (h e) c -> p h (e c)", h=2),
                in_=w.rearrange("(h p e) c -> p h (e c)", h=2, e=2),
            )
            return raw

        load_x(0)
        raw1 = load_mx_weight("w1", w1)
        raw0 = load_mx_weight("w0", w0)
        w2_sb = keep.tile([P, 2, MUL2], BF16, name="w2_sb")
        nc.sync.dma_start(out=w2_sb[:], in_=w2.rearrange("(m e) c -> m e c", e=2))
        for g in range(1, len(LOAD_GROUPS)):
            load_x(g)

        def mx_weight_tiles(name):
            grouped = keep.tile([P, MUL01, 4], BF16, name="grp_" + name, align_bytes=64)
            codes = keep.tile([P, MUL01], U32, name="codes_" + name, align_bytes=64)
            scales = keep.tile([P, MUL01], U8, name="scales_" + name, align_bytes=64)
            return grouped, codes, scales

        grouped1, codes1, scales1 = mx_weight_tiles("w1")
        grouped0, codes0, scales0 = mx_weight_tiles("w0")

        def quantise(grouped_flat, codes, scales):
            nc.vector.quantize_mx(out=codes[:].bitcast(FP8X4), scales=scales[:], in_=grouped_flat)

        sorted1 = {}
        mx_operands = {}
        plain_operands = {}

        def sort_block1(t):
            x_sb, k = x_tiles[t]
            by_component = stage.tile([P, D1 * MUL01], BF16, name="xs1")
            sorted1[t] = by_component
            nc.gpsimd.tensor_scalar(
                out=by_component[:].rearrange("p (i u) -> p i u", i=D1),
                in0=x_sb[:, k * COLS + OFF1:k * COLS + OFF2].rearrange("p (u i) -> p i u", i=D1),
                scalar1=1.0,
                scalar2=0.0,
                op0=MULT,
                op1=ADD,
            )

        def transposes(t):
            x_sb, k = x_tiles[t]
            pairs = x_sb[:].bitcast(F32)[:, k * PAIRS:(k + 1) * PAIRS]
            pairs1 = sorted1[t][:].bitcast(F32)

            x2T = stage.tile([P, 2 * D2 * P], BF16, name="xT2")
            plain_operands[t] = x2T
            bank_a = psum.tile([P, BANK], F32, name="tb2", tag="bank")
            for r in range(4):
                nc.tensor.transpose(bank_a[:, r * P:(r + 1) * P], pairs[:, OFF2 // 2 + r:PAIRS:D2], ident[:])
            bank_b = psum.tile([P, BANK], F32, name="tb3", tag="bank")
            nc.tensor.transpose(bank_b[:, 0:P], pairs[:, OFF2 // 2 + 4:PAIRS:D2], ident[:])
            nc.scalar.copy(
                x2T[:, 0:8 * P].rearrange("p (r e n) -> p r e n", r=4, e=2),
                bank_a[:].bitcast(BF16).rearrange("p (r n e) -> p r e n", r=4, e=2),
            )
            nc.vector.tensor_copy(
                out=x2T[:, 8 * P:10 * P].rearrange("p (e n) -> p e n", e=2),
                in_=bank_b[:].bitcast(BF16)[:, 0:2 * P].rearrange("p (n e) -> p e n", e=2),
            )

            grouped = stage.tile([P, OPERANDS * P * 4], BF16, name="grouped", align_bytes=64)
            grouped_pairs = grouped[:].bitcast(F32)
            for b in range(OPERANDS // 2):
                bank = psum.tile([P, BANK], F32, name="tb01", tag="bank")
                for s in (2 * b, 2 * b + 1):
                    for h in range(2):
                        if s == 0:
                            src = pairs[:, h * P:(h + 1) * P]
                        else:
                            src = pairs1[:, (2 * (s - 1) + h) * P:(2 * (s - 1) + h + 1) * P]
                        q = 2 * (s - 2 * b) + h
                        nc.tensor.transpose(bank[:, q * P:(q + 1) * P], src, ident[:])
                nc.vector.tensor_copy(
                    out=grouped_pairs[:, b * BANK:(b + 1) * BANK].rearrange("p (s n h) -> p s n h", s=2, h=2),
                    in_=bank[:].rearrange("p (s h n) -> p s n h", s=2, h=2),
                )
            codes = stage.tile([P, OPERANDS * P], U32, name="codes", align_bytes=64)
            scales = stage.tile([P, OPERANDS * P], U8, name="scales", align_bytes=64)
            mx_operands[t] = (grouped, codes, scales)

        def quantise_x(t):
            grouped, codes, scales = mx_operands[t]
            quantise(grouped[:], codes, scales)

        def products(t):
            grouped, codes, scales = mx_operands[t]
            x2T = plain_operands[t]
            o = outs.tile([P, COLS], F32, name="o")

            def mx_pass(acc, s, w_codes, w_scales):
                nc.tensor.matmul_mx(
                    out=acc,
                    lhsT=codes[:, s * P:(s + 1) * P].bitcast(FP8X4),
                    lhsT_scale=scales[:, s * P:(s + 1) * P],
                    rhs=w_codes.bitcast(FP8X4),
                    rhs_scale=w_scales,
                    start=True,
                    stop=True,
                )

            for c in range(MUL01 // CHUNK1):
                cols = slice(c * CHUNK1, (c + 1) * CHUNK1)
                acc1 = psum.tile([P, BANK], F32, name="acc1", tag="bank")
                for i in range(D1):
                    mx_pass(acc1[:, i * CHUNK1:(i + 1) * CHUNK1], 1 + i, codes1[:, cols], scales1[:, cols])
                lo = OFF1 + c * D1 * CHUNK1
                drain1[c](
                    o[:, lo:lo + D1 * CHUNK1].rearrange("p (w i) -> p w i", i=D1),
                    acc1[:, 0:D1 * CHUNK1].rearrange("p (i w) -> p w i", i=D1),
                    SCALE01,
                )
                if c == 1 and t + 1 < TILES:
                    quantise_x(t + 1)
            acc0 = psum.tile([P, BANK], F32, name="acc0", tag="bank")
            mx_pass(acc0[:], 0, codes0[:], scales0[:])
            vector_scaled(o[:, 0:OFF1], acc0[:], SCALE01)
            for c, (w_lo, w_n) in enumerate(CHUNKS2):
                acc2 = psum.tile([P, BANK], F32, name="acc2", tag="bank")
                for i in range(D2):
                    for e2 in range(2):
                        f = D2 * e2 + i
                        nc.tensor.matmul(
                            out=acc2[:, i * w_n:(i + 1) * w_n],
                            lhsT=x2T[:, f * P:(f + 1) * P],
                            rhs=w2_sb[:, e2, w_lo:w_lo + w_n],
                            start=(e2 == 0),
                            stop=(e2 == 1),
                        )
                drain2[c](
                    o[:, OFF2 + D2 * w_lo:OFF2 + D2 * (w_lo + w_n)].rearrange("p (w i) -> p w i", i=D2),
                    acc2[:, 0:D2 * w_n].rearrange("p (i w) -> p w i", i=D2),
                    SCALE2,
                )
            nc.sync.dma_start(out=out_rows[:, t * COLS:(t + 1) * COLS], in_=o[:])

        sort_block1(0)
        nc.vector.tensor_copy(out=grouped1[:], in_=raw1[:].rearrange("p t c -> p c t"))
        transposes(0)
        nc.scalar.copy(grouped0[:], raw0[:].rearrange("p t c -> p c t"))
        quantise(grouped1[:].rearrange("p c t -> p (c t)"), codes1, scales1)
        quantise_x(0)
        quantise(grouped0[:].rearrange("p c t -> p (c t)"), codes0, scales0)
        for t in range(TILES):
            if t + 1 < TILES:
                sort_block1(t + 1)
                transposes(t + 1)
            products(t)
